import numpy as np
import ml_dtypes


def mxq(x, axis, fmt="e4m3"):
    dtype, down = {"e4m3": (ml_dtypes.float8_e4m3fn, 7), "e5m2": (ml_dtypes.float8_e5m2, 14)}[fmt]
    v = np.moveaxis(np.asarray(x, np.float32).astype(ml_dtypes.bfloat16).astype(np.float64), axis, -1)
    blocks = v.reshape(v.shape[:-1] + (-1, 32))
    amax = np.abs(blocks).max(-1, keepdims=True)
    byte = np.maximum(np.where(amax > 0, np.frexp(amax)[1] - 1 + 127, 0) - down, 1)
    scale = np.exp2(byte - 127.0)
    codes = (blocks / scale).astype(np.float32).astype(dtype).astype(np.float64)
    return np.moveaxis((codes * scale).reshape(v.shape), -1, axis)


WIDE = False


def mx_kscale(k):
    if not WIDE:
        return np.ones(k)
    levels = np.array([20, -20, 10, -10, 0])
    a = np.random.permutation(np.resize(levels, k // 512 * 4)).reshape(k // 512, 4)
    idx = np.arange(k)
    return np.exp2(a[idx // 512, idx % 128 // 32])


BF16 = ml_dtypes.bfloat16


def bf(x):
    return np.asarray(x, np.float32).astype(BF16)


def f64(x):
    return np.asarray(x).astype(np.float64)


B, N, F, O, E, K = 4, 256, 128, 512, 16, 3


def setup_inputs():
    se = np.asarray(mx_kscale(E * O)).reshape(E, O)[:, 0]
    x_g = np.random.standard_normal((B, K, N, F))
    emb = np.random.standard_normal((B, N, E)) * se
    weights_pool = np.random.standard_normal((E, K, F, O)) * 0.5 / np.sqrt(K * F) / se[:, None, None, None]
    bias_pool = np.random.standard_normal((E, O)) * 0.3 / se[:, None]
    g = np.random.standard_normal((B, N, O)) * np.exp2(np.random.randint(-12, 1, (B, N, 1))) * 64.0
    return {"x_g": bf(x_g), "emb": bf(emb), "weights_pool": bf(weights_pool), "bias_pool": bf(bias_pool),
            "grad_out": bf(g)}


def reference(x_g, emb, weights_pool, bias_pool, grad_out):
    e, w, g = f64(emb), f64(weights_pool), f64(grad_out)
    gz = (e[:, :, :, None] * g[:, :, None, :]).reshape(B * N, E * O)
    wt = w.transpose(1, 2, 0, 3).reshape(K * F, E * O)
    gx = mxq(gz, 1, "e5m2") @ mxq(wt, 1, "e4m3").T
    return gx.reshape(B, N, K, F).transpose(0, 2, 1, 3)

@@ -1,0 +1,200 @@
+from contextlib import ExitStack
+
+import concourse.mybir as mybir
+from concourse.masks import make_identity
+
+BF16 = mybir.dt.bfloat16
+F32 = mybir.dt.float32
+U32 = mybir.dt.uint32
+U8 = mybir.dt.uint8
+E4M3_X4 = mybir.dt.float8_e4m3fn_x4
+E5M2_X4 = mybir.dt.float8_e5m2_x4
+
+P = 128
+PACK = 4
+N_EMB = 16
+N_CHEB = 3
+N_OUT = 512
+N_TILES = 8
+HALF_TILES = 4
+HALF = HALF_TILES * P
+ROUNDS_PER_HALF = N_EMB // 2
+N_ROUNDS = 2 * ROUNDS_PER_HALF
+BLOCKS_PER_BANK = 2
+WEIGHT_BANKS_PER_ROUND = 3
+
+FLOPS = 2 * 1024 * 384 * 8192
+BYTES = 2 * (1024 * 16 + 16 * 3 * 128 * 512 + 1024 * 512) + 4 * 1024 * 384
+
+
+def tile_dygcn_pb_k_kernel(tc, x_g, emb, weights_pool, bias_pool, grad_out, out):
+    nc = tc.nc
+    with ExitStack() as ctx:
+        keep = ctx.enter_context(tc.tile_pool(name="keep", bufs=1))
+        ring = ctx.enter_context(tc.tile_pool(name="ring", bufs=3))
+        sum_banks = ctx.enter_context(tc.psum_pool(name="sum_banks", bufs=1))
+        turn_banks = ctx.enter_context(tc.psum_pool(name="turn_banks", bufs=5))
+
+        emb_rows = keep.tile([P, N_TILES * N_EMB], BF16)
+        g_rows = keep.tile([P, N_TILES, N_OUT], BF16)
+        w_rows = keep.tile([P, N_EMB * N_CHEB, N_OUT], BF16)
+        g_view = grad_out.rearrange("b (s p) o -> p (b s) o", p=P)
+        w_view = weights_pool.rearrange("e k f o -> f (e k) o")
+        nc.sync.dma_start(
+            out=emb_rows[:].rearrange("p (i e) -> p i e", e=N_EMB),
+            in_=emb.rearrange("b (s p) e -> p (b s) e", p=P),
+        )
+        nc.sync.dma_start(out=g_rows[:, :HALF_TILES, :], in_=g_view[:, :HALF_TILES, :])
+        for pair in range(ROUNDS_PER_HALF):
+            blocks = slice(pair * 2 * N_CHEB, (pair + 1) * 2 * N_CHEB)
+            nc.sync.dma_start(out=w_rows[:, blocks, :], in_=w_view[:, blocks, :])
+        nc.sync.dma_start(out=g_rows[:, HALF_TILES:, :], in_=g_view[:, HALF_TILES:, :])
+
+        identity = keep.tile([P, P], F32)
+        make_identity(nc, identity[:])
+
+        emb_pairs = keep.tile([P, N_TILES * N_EMB * 2], BF16)
+        nc.vector.tensor_copy(
+            out=emb_pairs[:].rearrange("p (c i) -> p c i", i=2),
+            in_=emb_rows[:].unsqueeze(2).to_broadcast([P, N_TILES * N_EMB, 2]),
+        )
+        emb_words = emb_pairs[:].bitcast(F32)
+
+        g_cols = keep.tile([P, 2, HALF * PACK], BF16)
+        w_codes = keep.tile([P, N_EMB * N_CHEB * P], U32, align_bytes=64)
+        w_scales = keep.tile([P, N_EMB * N_CHEB * P], U8, align_bytes=64)
+
+        def turn_rows(bank, rows):
+            words = rows.bitcast(F32)
+            for u in range(2):
+                nc.tensor.transpose(bank[:, u, :], words[:, u * P : (u + 1) * P], identity[:])
+
+        def turn_gradient(half):
+            for bank_index in range(HALF_TILES // BLOCKS_PER_BANK):
+                bank = turn_banks.tile([P, BLOCKS_PER_BANK, 2, P], F32, tag="turn")
+                for c in range(BLOCKS_PER_BANK):
+                    turn_rows(bank[:, c], g_rows[:, half * HALF_TILES + bank_index * BLOCKS_PER_BANK + c, :])
+                width = BLOCKS_PER_BANK * P * PACK
+                nc.scalar.copy(
+                    out=g_cols[:, half, bank_index * width : (bank_index + 1) * width]
+                    .bitcast(F32)
+                    .rearrange("p (c t u) -> p c t u", c=BLOCKS_PER_BANK, u=2),
+                    in_=bank[:].rearrange("p c u t -> p c t u"),
+                )
+
+        def turn_weights(pair):
+            grouped_tiles = []
+            for bank_index in range(WEIGHT_BANKS_PER_ROUND):
+                bank = turn_banks.tile([P, BLOCKS_PER_BANK, 2, P], F32, tag="turn")
+                for c in range(BLOCKS_PER_BANK):
+                    block = (pair * WEIGHT_BANKS_PER_ROUND + bank_index) * BLOCKS_PER_BANK + c
+                    turn_rows(bank[:, c], w_rows[:, block, :])
+                grouped = ring.tile(
+                    [P, BLOCKS_PER_BANK * P * PACK],
+                    BF16,
+                    tag="w_grouped",
+                    bufs=2 * WEIGHT_BANKS_PER_ROUND,
+                    align_bytes=64,
+                )
+                nc.scalar.copy(
+                    out=grouped[:].bitcast(F32).rearrange("p (c f u) -> p c f u", c=BLOCKS_PER_BANK, u=2),
+                    in_=bank[:].rearrange("p c u f -> p c f u"),
+                )
+                grouped_tiles.append(grouped)
+            return grouped_tiles
+
+        def quantise_weights(pair, grouped_tiles):
+            for bank_index in range(WEIGHT_BANKS_PER_ROUND):
+                first = (pair * WEIGHT_BANKS_PER_ROUND + bank_index) * BLOCKS_PER_BANK * P
+                cols = slice(first, first + BLOCKS_PER_BANK * P)
+                nc.vector.quantize_mx(
+                    out=w_codes[:, cols].bitcast(E4M3_X4),
+                    scales=w_scales[:, cols],
+                    in_=grouped_tiles[bank_index][:],
+                )
+
+        def spread_embedding(half, pair):
+            spread = ring.tile([P, 2, HALF * 2], BF16, tag="spread")
+            for c in range(2):
+                bank = turn_banks.tile([P, HALF_TILES, P], F32, tag="turn")
+                for i in range(HALF_TILES):
+                    column = (half * HALF_TILES + i) * N_EMB + 2 * pair + c
+                    nc.tensor.transpose(
+                        bank[:, i, :], emb_words[:, column : column + 1].to_broadcast([P, P]), identity[:]
+                    )
+                nc.scalar.copy(out=spread[:, c, :].bitcast(F32), in_=bank[:].rearrange("p i t -> p (i t)"))
+            return spread
+
+        def gate_and_quantise(half, spread):
+            gated = ring.tile([P, 2, HALF * PACK], BF16, tag="gated", align_bytes=64)
+            codes = ring.tile([P, 2, HALF], U32, tag="codes", align_bytes=64)
+            scales = ring.tile([P, 2, HALF], U8, tag="scales", align_bytes=64)
+            for c in range(2):
+                nc.vector.tensor_tensor(
+                    out=gated[:, c, :].rearrange("p (t u i) -> p t u i", u=2, i=2),
+                    in0=g_cols[:, half, :].rearrange("p (t u i) -> p t u i", u=2, i=2),
+                    in1=spread[:, c, :]
+                    .rearrange("p (t i) -> p t i", i=2)
+                    .unsqueeze(2)
+                    .to_broadcast([P, HALF, 2, 2]),
+                    op=mybir.AluOpType.mult,
+                )
+            for c in range(2):
+                nc.vector.quantize_mx(out=codes[:, c, :].bitcast(E5M2_X4), scales=scales[:, c, :], in_=gated[:, c, :])
+            return codes, scales
+
+        def multiply(pair, codes, scales, sums):
+            for c in range(2):
+                e = 2 * pair + c
+                for k in range(N_CHEB):
+                    cols = slice((e * N_CHEB + k) * P, (e * N_CHEB + k + 1) * P)
+                    nc.tensor.matmul_mx(
+                        out=sums[k][:],
+                        lhsT=w_codes[:, cols].bitcast(E4M3_X4),
+                        lhsT_scale=w_scales[:, cols],
+                        rhs=codes[:, c, :].bitcast(E5M2_X4),
+                        rhs_scale=scales[:, c, :],
+                        start=(e == 0),
+                        stop=(e == N_EMB - 1),
+                    )
+
+        def store_half(half, sums):
+            feature_rows = []
+            for k in range(N_CHEB):
+                rows = ring.tile([P, HALF], F32, name="feature_rows%d" % k, tag="feature_rows%d" % k, bufs=1)
+                nc.scalar.copy(out=rows[:], in_=sums[k][:])
+                feature_rows.append(rows)
+            for i in range(HALF_TILES):
+                bank = turn_banks.tile([P, N_CHEB, P], F32, tag="turn")
+                for k in range(N_CHEB):
+                    nc.tensor.transpose(bank[:, k, :], feature_rows[k][:, i * P : (i + 1) * P], identity[:])
+                token_rows = ring.tile([P, N_CHEB, P], F32, tag="token_rows")
+                nc.scalar.copy(out=token_rows[:], in_=bank[:])
+                b, s = divmod(half * HALF_TILES + i, 2)
+                nc.sync.dma_start(
+                    out=out[b, :, s * P : (s + 1) * P, :].rearrange("k n f -> n k f"), in_=token_rows[:]
+                )
+
+        spread = spread_embedding(0, 0)
+        turn_gradient(0)
+        grouped_tiles = turn_weights(0)
+        sums = []
+        for r in range(N_ROUNDS):
+            half, pair = divmod(r, ROUNDS_PER_HALF)
+            if pair == 0:
+                sums = [sum_banks.tile([P, HALF], F32, name="sum%d" % k, tag="sum%d" % k) for k in range(N_CHEB)]
+            this_spread = spread
+            this_grouped = grouped_tiles
+            if r + 1 < N_ROUNDS:
+                next_half, next_pair = divmod(r + 1, ROUNDS_PER_HALF)
+                if next_half == 0:
+                    grouped_tiles = turn_weights(next_pair)
+                elif next_pair == 0:
+                    turn_gradient(next_half)
+                spread = spread_embedding(next_half, next_pair)
+            codes, scales = gate_and_quantise(half, this_spread)
+            if half == 0:
+                quantise_weights(pair, this_grouped)
+            multiply(pair, codes, scales, sums)
+            if pair == ROUNDS_PER_HALF - 1:
+                store_half(half, sums)

@@ -114,15 +114,17 @@ def tile_dygcn_pb_k_kernel(tc, x_g, emb, weights_pool, bias_pool, grad_out, out)
                 )
 
         def spread_embedding(half, pair):
-            spread = ring.tile([P, 2, HALF * 2], BF16, tag="spread")
+            spread = []
             for c in range(2):
-                bank = turn_banks.tile([P, HALF_TILES, P], F32, tag="turn")
+                bank = turn_banks.tile([P, HALF], F32, tag="turn")
                 for i in range(HALF_TILES):
                     column = (half * HALF_TILES + i) * N_EMB + 2 * pair + c
                     nc.tensor.transpose(
-                        bank[:, i, :], emb_words[:, column : column + 1].to_broadcast([P, P]), identity[:]
+                        bank[:, i * P : (i + 1) * P],
+                        emb_words[:, column : column + 1].to_broadcast([P, P]),
+                        identity[:],
                     )
-                nc.scalar.copy(out=spread[:, c, :].bitcast(F32), in_=bank[:].rearrange("p i t -> p (i t)"))
+                spread.append(bank)
             return spread
 
         def gate_and_quantise(half, spread):
@@ -133,7 +135,8 @@ def tile_dygcn_pb_k_kernel(tc, x_g, emb, weights_pool, bias_pool, grad_out, out)
                 nc.vector.tensor_tensor(
                     out=gated[:, c, :].rearrange("p (t u i) -> p t u i", u=2, i=2),
                     in0=g_cols[:, half, :].rearrange("p (t u i) -> p t u i", u=2, i=2),
-                    in1=spread[:, c, :]
+                    in1=spread[c][:]
+                    .bitcast(BF16)
                     .rearrange("p (t i) -> p t i", i=2)
                     .unsqueeze(2)
                     .to_broadcast([P, HALF, 2, 2]),

@@ -18,6 +18,7 @@ N_OUT = 512
 N_TILES = 8
 HALF_TILES = 4
 HALF = HALF_TILES * P
+VECTOR_TILES = 3
 ROUNDS_PER_HALF = N_EMB // 2
 N_ROUNDS = 2 * ROUNDS_PER_HALF
 BLOCKS_PER_BANK = 2
@@ -59,8 +60,10 @@ def tile_dygcn_pb_k_kernel(tc, x_g, emb, weights_pool, bias_pool, grad_out, out)
             in_=emb_rows[:].unsqueeze(2).to_broadcast([P, N_TILES * N_EMB, 2]),
         )
         emb_words = emb_pairs[:].bitcast(F32)
+        emb_scales = keep.tile([P, N_TILES * N_EMB], F32)
+        nc.scalar.copy(out=emb_scales[:], in_=emb_rows[:])
 
-        g_cols = keep.tile([P, 2, HALF * PACK], BF16)
+        g_cols = keep.tile([P, 2, VECTOR_TILES * P * PACK], BF16)
         w_codes = keep.tile([P, N_EMB * N_CHEB * P], U32, align_bytes=64)
         w_scales = keep.tile([P, N_EMB * N_CHEB * P], U8, align_bytes=64)
 
@@ -70,16 +73,14 @@ def tile_dygcn_pb_k_kernel(tc, x_g, emb, weights_pool, bias_pool, grad_out, out)
                 nc.tensor.transpose(bank[:, u, :], words[:, u * P : (u + 1) * P], identity[:])
 
         def turn_gradient(half):
-            for bank_index in range(HALF_TILES // BLOCKS_PER_BANK):
-                bank = turn_banks.tile([P, BLOCKS_PER_BANK, 2, P], F32, tag="turn")
-                for c in range(BLOCKS_PER_BANK):
-                    turn_rows(bank[:, c], g_rows[:, half * HALF_TILES + bank_index * BLOCKS_PER_BANK + c, :])
-                width = BLOCKS_PER_BANK * P * PACK
+            for i in range(VECTOR_TILES):
+                bank = turn_banks.tile([P, 2, P], F32, tag="turn")
+                turn_rows(bank, g_rows[:, half * HALF_TILES + i, :])
                 nc.scalar.copy(
-                    out=g_cols[:, half, bank_index * width : (bank_index + 1) * width]
+                    out=g_cols[:, half, i * P * PACK : (i + 1) * P * PACK]
                     .bitcast(F32)
-                    .rearrange("p (c t u) -> p c t u", c=BLOCKS_PER_BANK, u=2),
-                    in_=bank[:].rearrange("p c u t -> p c t u"),
+                    .rearrange("p (t u) -> p t u", u=2),
+                    in_=bank[:].rearrange("p u t -> p t u"),
                 )
 
         def turn_weights(pair):
@@ -113,11 +114,33 @@ def tile_dygcn_pb_k_kernel(tc, x_g, emb, weights_pool, bias_pool, grad_out, out)
                     in_=grouped_tiles[bank_index][:],
                 )
 
+        def gate_on_scalar(half, pair, gated):
+            for i in range(VECTOR_TILES, HALF_TILES):
+                tile_index = half * HALF_TILES + i
+                scaled = ring.tile([P, 2, N_OUT], BF16, tag="scaled")
+                for c in range(2):
+                    column = tile_index * N_EMB + 2 * pair + c
+                    nc.scalar.activation(
+                        out=scaled[:, c, :],
+                        in_=g_rows[:, tile_index, :],
+                        func=mybir.ActivationFunctionType.Copy,
+                        scale=emb_scales[:, column : column + 1],
+                    )
+                bank = turn_banks.tile([P, 2, 2, P], F32, tag="turn")
+                for c in range(2):
+                    turn_rows(bank[:, c], scaled[:, c, :])
+                nc.scalar.copy(
+                    out=gated[:, :, i * P * PACK : (i + 1) * P * PACK]
+                    .bitcast(F32)
+                    .rearrange("p c (t u) -> p c t u", u=2),
+                    in_=bank[:].rearrange("p c u t -> p c t u"),
+                )
+
         def spread_embedding(half, pair):
             spread = []
             for c in range(2):
-                bank = turn_banks.tile([P, HALF], F32, tag="turn")
-                for i in range(HALF_TILES):
+                bank = turn_banks.tile([P, VECTOR_TILES * P], F32, tag="turn")
+                for i in range(VECTOR_TILES):
                     column = (half * HALF_TILES + i) * N_EMB + 2 * pair + c
                     nc.tensor.transpose(
                         bank[:, i * P : (i + 1) * P],
@@ -127,19 +150,30 @@ def tile_dygcn_pb_k_kernel(tc, x_g, emb, weights_pool, bias_pool, grad_out, out)
                 spread.append(bank)
             return spread
 
-        def gate_and_quantise(half, spread):
+        def prepare(r):
+            half, pair = divmod(r, ROUNDS_PER_HALF)
             gated = ring.tile([P, 2, HALF * PACK], BF16, tag="gated", align_bytes=64)
+            if pair == 0:
+                turn_gradient(half)
+            spread = spread_embedding(half, pair)
+            gate_on_scalar(half, pair, gated)
+            grouped_tiles = []
+            if half == 0:
+                grouped_tiles = turn_weights(pair)
+            return gated, grouped_tiles, spread
+
+        def gate_and_quantise(half, gated, spread):
             codes = ring.tile([P, 2, HALF], U32, tag="codes", align_bytes=64)
             scales = ring.tile([P, 2, HALF], U8, tag="scales", align_bytes=64)
             for c in range(2):
                 nc.vector.tensor_tensor(
-                    out=gated[:, c, :].rearrange("p (t u i) -> p t u i", u=2, i=2),
+                    out=gated[:, c, : VECTOR_TILES * P * PACK].rearrange("p (t u i) -> p t u i", u=2, i=2),
                     in0=g_cols[:, half, :].rearrange("p (t u i) -> p t u i", u=2, i=2),
                     in1=spread[c][:]
                     .bitcast(BF16)
                     .rearrange("p (t i) -> p t i", i=2)
                     .unsqueeze(2)
-                    .to_broadcast([P, HALF, 2, 2]),
+                    .to_broadcast([P, VECTOR_TILES * P, 2, 2]),
                     op=mybir.AluOpType.mult,
                 )
             for c in range(2):
@@ -178,26 +212,18 @@ def tile_dygcn_pb_k_kernel(tc, x_g, emb, weights_pool, bias_pool, grad_out, out)
                     out=out[b, :, s * P : (s + 1) * P, :].rearrange("k n f -> n k f"), in_=token_rows[:]
                 )
 
-        spread = spread_embedding(0, 0)
-        turn_gradient(0)
-        grouped_tiles = turn_weights(0)
+        prepared = prepare(0)
         sums = []
         for r in range(N_ROUNDS):
             half, pair = divmod(r, ROUNDS_PER_HALF)
             if pair == 0:
                 sums = [sum_banks.tile([P, HALF], F32, name="sum%d" % k, tag="sum%d" % k) for k in range(N_CHEB)]
-            this_spread = spread
-            this_grouped = grouped_tiles
+            gated, grouped_tiles, spread = prepared
             if r + 1 < N_ROUNDS:
-                next_half, next_pair = divmod(r + 1, ROUNDS_PER_HALF)
-                if next_half == 0:
-                    grouped_tiles = turn_weights(next_pair)
-                elif next_pair == 0:
-                    turn_gradient(next_half)
-                spread = spread_embedding(next_half, next_pair)
-            codes, scales = gate_and_quantise(half, this_spread)
+                prepared = prepare(r + 1)
+            codes, scales = gate_and_quantise(half, gated, spread)
             if half == 0:
-                quantise_weights(pair, this_grouped)
+                quantise_weights(pair, grouped_tiles)
             multiply(pair, codes, scales, sums)
             if pair == ROUNDS_PER_HALF - 1:
                 store_half(half, sums)

@@ -45,7 +45,8 @@ def tile_dygcn_pb_k_kernel(tc, x_g, emb, weights_pool, bias_pool, grad_out, out)
             out=emb_rows[:].rearrange("p (i e) -> p i e", e=N_EMB),
             in_=emb.rearrange("b (s p) e -> p (b s) e", p=P),
         )
-        nc.sync.dma_start(out=g_rows[:, :HALF_TILES, :], in_=g_view[:, :HALF_TILES, :])
+        for i in range(HALF_TILES):
+            nc.sync.dma_start(out=g_rows[:, i, :], in_=g_view[:, i, :])
         for pair in range(ROUNDS_PER_HALF):
             blocks = slice(pair * 2 * N_CHEB, (pair + 1) * 2 * N_CHEB)
             nc.sync.dma_start(out=w_rows[:, blocks, :], in_=w_view[:, blocks, :])
@@ -76,7 +77,8 @@ def tile_dygcn_pb_k_kernel(tc, x_g, emb, weights_pool, bias_pool, grad_out, out)
             for i in range(VECTOR_TILES):
                 bank = turn_banks.tile([P, 2, P], F32, tag="turn")
                 turn_rows(bank, g_rows[:, half * HALF_TILES + i, :])
-                nc.scalar.copy(
+                copy_out = nc.vector.tensor_copy if half == 0 else nc.scalar.copy
+                copy_out(
                     out=g_cols[:, half, i * P * PACK : (i + 1) * P * PACK]
                     .bitcast(F32)
                     .rearrange("p (t u) -> p t u", u=2),
@@ -153,9 +155,9 @@ def tile_dygcn_pb_k_kernel(tc, x_g, emb, weights_pool, bias_pool, grad_out, out)
         def prepare(r):
             half, pair = divmod(r, ROUNDS_PER_HALF)
             gated = ring.tile([P, 2, HALF * PACK], BF16, tag="gated", align_bytes=64)
+            spread = spread_embedding(half, pair)
             if pair == 0:
                 turn_gradient(half)
-            spread = spread_embedding(half, pair)
             gate_on_scalar(half, pair, gated)
             grouped_tiles = []
             if half == 0:
@@ -195,25 +197,43 @@ def tile_dygcn_pb_k_kernel(tc, x_g, emb, weights_pool, bias_pool, grad_out, out)
                         stop=(e == N_EMB - 1),
                     )
 
-        def store_half(half, sums):
+        def empty_sums(sums):
             feature_rows = []
             for k in range(N_CHEB):
                 rows = ring.tile([P, HALF], F32, name="feature_rows%d" % k, tag="feature_rows%d" % k, bufs=1)
                 nc.scalar.copy(out=rows[:], in_=sums[k][:])
                 feature_rows.append(rows)
-            for i in range(HALF_TILES):
-                bank = turn_banks.tile([P, N_CHEB, P], F32, tag="turn")
-                for k in range(N_CHEB):
-                    nc.tensor.transpose(bank[:, k, :], feature_rows[k][:, i * P : (i + 1) * P], identity[:])
-                token_rows = ring.tile([P, N_CHEB, P], F32, tag="token_rows")
-                nc.scalar.copy(out=token_rows[:], in_=bank[:])
-                b, s = divmod(half * HALF_TILES + i, 2)
-                nc.sync.dma_start(
-                    out=out[b, :, s * P : (s + 1) * P, :].rearrange("k n f -> n k f"), in_=token_rows[:]
-                )
+            return feature_rows
+
+        def store_tile(half, i, feature_rows):
+            bank = turn_banks.tile([P, N_CHEB, P], F32, tag="turn")
+            for k in range(N_CHEB):
+                nc.tensor.transpose(bank[:, k, :], feature_rows[k][:, i * P : (i + 1) * P], identity[:])
+            token_rows = ring.tile([P, N_CHEB, P], F32, tag="token_rows")
+            nc.scalar.copy(out=token_rows[:], in_=bank[:])
+            b, s = divmod(half * HALF_TILES + i, 2)
+            nc.sync.dma_start(out=out[b, :, s * P : (s + 1) * P, :].rearrange("k n f -> n k f"), in_=token_rows[:])
+
+        def store_last_half(sums):
+            first_copy = [nc.scalar.copy, nc.vector.tensor_copy, nc.scalar.copy]
+            second_copy = [nc.vector.tensor_copy, nc.scalar.copy, nc.vector.tensor_copy]
+            for k in range(N_CHEB):
+                rows = ring.tile([P, HALF], F32, name="feature_rows%d" % k, tag="feature_rows%d" % k, bufs=1)
+                first_copy[k](out=rows[:], in_=sums[k][:])
+                bank = turn_banks.tile([P, HALF_TILES, P], F32, tag="turn")
+                for i in range(HALF_TILES):
+                    nc.tensor.transpose(bank[:, i, :], rows[:, i * P : (i + 1) * P], identity[:])
+                token_rows = ring.tile([P, HALF_TILES, P], F32, tag="last_rows")
+                second_copy[k](out=token_rows[:], in_=bank[:])
+                for j in range(2):
+                    nc.sync.dma_start(
+                        out=out[2 + j, k, :, :].rearrange("(s n) f -> n s f", s=2),
+                        in_=token_rows[:, 2 * j : 2 * j + 2, :],
+                    )
 
         prepared = prepare(0)
         sums = []
+        feature_rows = []
         for r in range(N_ROUNDS):
             half, pair = divmod(r, ROUNDS_PER_HALF)
             if pair == 0:
@@ -221,9 +241,12 @@ def tile_dygcn_pb_k_kernel(tc, x_g, emb, weights_pool, bias_pool, grad_out, out)
             gated, grouped_tiles, spread = prepared
             if r + 1 < N_ROUNDS:
                 prepared = prepare(r + 1)
+            if half == 1 and 1 <= pair <= HALF_TILES:
+                store_tile(0, pair - 1, feature_rows)
             codes, scales = gate_and_quantise(half, gated, spread)
             if half == 0:
                 quantise_weights(pair, grouped_tiles)
             multiply(pair, codes, scales, sums)
-            if pair == ROUNDS_PER_HALF - 1:
-                store_half(half, sums)
+            if r == ROUNDS_PER_HALF - 1:
+                feature_rows = empty_sums(sums)
+        store_last_half(sums)

@@ -19,6 +19,8 @@ N_TILES = 8
 HALF_TILES = 4
 HALF = HALF_TILES * P
 VECTOR_TILES = 3
+PE_SPREAD_ROUNDS = 2
+LOAD_AHEAD = 3
 ROUNDS_PER_HALF = N_EMB // 2
 N_ROUNDS = 2 * ROUNDS_PER_HALF
 BLOCKS_PER_BANK = 2
@@ -47,10 +49,12 @@ def tile_dygcn_pb_k_kernel(tc, x_g, emb, weights_pool, bias_pool, grad_out, out)
         )
         for i in range(HALF_TILES):
             nc.sync.dma_start(out=g_rows[:, i, :], in_=g_view[:, i, :])
-        for pair in range(ROUNDS_PER_HALF):
+
+        def load_weights(pair):
             blocks = slice(pair * 2 * N_CHEB, (pair + 1) * 2 * N_CHEB)
             nc.sync.dma_start(out=w_rows[:, blocks, :], in_=w_view[:, blocks, :])
-        nc.sync.dma_start(out=g_rows[:, HALF_TILES:, :], in_=g_view[:, HALF_TILES:, :])
+
+        load_weights(0)
 
         identity = keep.tile([P, P], F32)
         make_identity(nc, identity[:])
@@ -63,6 +67,34 @@ def tile_dygcn_pb_k_kernel(tc, x_g, emb, weights_pool, bias_pool, grad_out, out)
         emb_words = emb_pairs[:].bitcast(F32)
         emb_scales = keep.tile([P, N_TILES * N_EMB], F32)
         nc.scalar.copy(out=emb_scales[:], in_=emb_rows[:])
+
+        emb_pairs_by_e = keep.tile([P, N_EMB * N_TILES * 2], BF16)
+        nc.vector.tensor_copy(
+            out=emb_pairs_by_e[:].rearrange("p (e i w) -> p e i w", e=N_EMB, w=2),
+            in_=emb_rows[:]
+            .rearrange("p (i e) -> p e i", e=N_EMB)
+            .unsqueeze(3)
+            .to_broadcast([P, N_EMB, N_TILES, 2]),
+        )
+        emb_bank = turn_banks.tile([P, P], F32, tag="turn")
+        nc.tensor.transpose(emb_bank[:], emb_pairs_by_e[:].bitcast(F32), identity[:])
+        emb_cols = keep.tile([P, P], F32)
+        nc.vector.tensor_copy(out=emb_cols[:], in_=emb_bank[:])
+        parked = out[3, 2, P : 2 * P, :]
+        nc.sync.dma_start(out=parked, in_=emb_cols[:])
+        parked_by_e = parked.rearrange("(e i) t -> e i t", i=N_TILES)
+        for pair in range(1, 4):
+            load_weights(pair)
+
+        def load_spread(r):
+            half, pair = divmod(r, ROUNDS_PER_HALF)
+            words = ring.tile([P, 2, VECTOR_TILES * P], F32, tag="spread_words", bufs=5)
+            first = half * HALF_TILES
+            nc.sync.dma_start(
+                out=words[:].rearrange("p c (i t) -> p c i t", i=VECTOR_TILES),
+                in_=parked_by_e[2 * pair : 2 * pair + 2, first : first + VECTOR_TILES, :].partition_broadcast(P),
+            )
+            return [words[:, 0, :], words[:, 1, :]]
 
         g_cols = keep.tile([P, 2, VECTOR_TILES * P * PACK], BF16)
         w_codes = keep.tile([P, N_EMB * N_CHEB * P], U32, align_bytes=64)
@@ -149,13 +181,13 @@ def tile_dygcn_pb_k_kernel(tc, x_g, emb, weights_pool, bias_pool, grad_out, out)
                         emb_words[:, column : column + 1].to_broadcast([P, P]),
                         identity[:],
                     )
-                spread.append(bank)
+                spread.append(bank[:])
             return spread
 
         def prepare(r):
             half, pair = divmod(r, ROUNDS_PER_HALF)
             gated = ring.tile([P, 2, HALF * PACK], BF16, tag="gated", align_bytes=64)
-            spread = spread_embedding(half, pair)
+            spread = spread_embedding(half, pair) if r < PE_SPREAD_ROUNDS else loaded[r]
             if pair == 0:
                 turn_gradient(half)
             gate_on_scalar(half, pair, gated)
@@ -171,7 +203,7 @@ def tile_dygcn_pb_k_kernel(tc, x_g, emb, weights_pool, bias_pool, grad_out, out)
                 nc.vector.tensor_tensor(
                     out=gated[:, c, : VECTOR_TILES * P * PACK].rearrange("p (t u i) -> p t u i", u=2, i=2),
                     in0=g_cols[:, half, :].rearrange("p (t u i) -> p t u i", u=2, i=2),
-                    in1=spread[c][:]
+                    in1=spread[c]
                     .bitcast(BF16)
                     .rearrange("p (t i) -> p t i", i=2)
                     .unsqueeze(2)
@@ -231,6 +263,9 @@ def tile_dygcn_pb_k_kernel(tc, x_g, emb, weights_pool, bias_pool, grad_out, out)
                         in_=token_rows[:, 2 * j : 2 * j + 2, :],
                     )
 
+        loaded = {}
+        for r in range(PE_SPREAD_ROUNDS, 1 + LOAD_AHEAD):
+            loaded[r] = load_spread(r)
         prepared = prepare(0)
         sums = []
         feature_rows = []
@@ -239,6 +274,12 @@ def tile_dygcn_pb_k_kernel(tc, x_g, emb, weights_pool, bias_pool, grad_out, out)
             if pair == 0:
                 sums = [sum_banks.tile([P, HALF], F32, name="sum%d" % k, tag="sum%d" % k) for k in range(N_CHEB)]
             gated, grouped_tiles, spread = prepared
+            if r + 4 < ROUNDS_PER_HALF:
+                load_weights(r + 4)
+            if r + 4 == ROUNDS_PER_HALF:
+                nc.sync.dma_start(out=g_rows[:, HALF_TILES:, :], in_=g_view[:, HALF_TILES:, :])
+            if r + 1 + LOAD_AHEAD < N_ROUNDS:
+                loaded[r + 1 + LOAD_AHEAD] = load_spread(r + 1 + LOAD_AHEAD)
             if r + 1 < N_ROUNDS:
                 prepared = prepare(r + 1)
             if half == 1 and 1 <= pair <= HALF_TILES:

@@ -19,7 +19,7 @@ N_TILES = 8
 HALF_TILES = 4
 HALF = HALF_TILES * P
 VECTOR_TILES = 3
-PE_SPREAD_ROUNDS = 2
+PE_SPREAD_ROUNDS = 5
 LOAD_AHEAD = 3
 ROUNDS_PER_HALF = N_EMB // 2
 N_ROUNDS = 2 * ROUNDS_PER_HALF
@@ -278,7 +278,7 @@ def tile_dygcn_pb_k_kernel(tc, x_g, emb, weights_pool, bias_pool, grad_out, out)
                 load_weights(r + 4)
             if r + 4 == ROUNDS_PER_HALF:
                 nc.sync.dma_start(out=g_rows[:, HALF_TILES:, :], in_=g_view[:, HALF_TILES:, :])
-            if r + 1 + LOAD_AHEAD < N_ROUNDS:
+            if PE_SPREAD_ROUNDS <= r + 1 + LOAD_AHEAD < N_ROUNDS:
                 loaded[r + 1 + LOAD_AHEAD] = load_spread(r + 1 + LOAD_AHEAD)
             if r + 1 < N_ROUNDS:
                 prepared = prepare(r + 1)

@@ -7,6 +7,7 @@ BF16 = mybir.dt.bfloat16
 F32 = mybir.dt.float32
 U32 = mybir.dt.uint32
 U8 = mybir.dt.uint8
+I32 = mybir.dt.int32
 E4M3_X4 = mybir.dt.float8_e4m3fn_x4
 E5M2_X4 = mybir.dt.float8_e5m2_x4
 
@@ -97,8 +98,10 @@ def tile_dygcn_pb_k_kernel(tc, x_g, emb, weights_pool, bias_pool, grad_out, out)
             return [words[:, 0, :], words[:, 1, :]]
 
         g_cols = keep.tile([P, 2, VECTOR_TILES * P * PACK], BF16)
-        w_codes = keep.tile([P, N_EMB * N_CHEB * P], U32, align_bytes=64)
-        w_scales = keep.tile([P, N_EMB * N_CHEB * P], U8, align_bytes=64)
+        w_codes = keep.tile([P, (N_EMB * N_CHEB + 1) * P], U32, align_bytes=64)
+        w_scales = keep.tile([P, (N_EMB * N_CHEB + 1) * P], U8, align_bytes=64)
+        nc.vector.memset(w_codes[:, N_EMB * N_CHEB * P :].bitcast(I32), 0)
+        nc.vector.memset(w_scales[:, N_EMB * N_CHEB * P :].bitcast(I32), 0)
 
         def turn_rows(bank, rows):
             words = rows.bitcast(F32)
@@ -229,6 +232,22 @@ def tile_dygcn_pb_k_kernel(tc, x_g, emb, weights_pool, bias_pool, grad_out, out)
                         stop=(e == N_EMB - 1),
                     )
 
+        def multiply_by_tokens(pair, codes, scales, token_sums):
+            for c in range(2):
+                e = 2 * pair + c
+                w_cols = slice(e * N_CHEB * P, (e * N_CHEB + PACK) * P)
+                for i in range(HALF_TILES):
+                    cols = slice(i * P, (i + 1) * P)
+                    nc.tensor.matmul_mx(
+                        out=token_sums[i][:],
+                        lhsT=codes[:, c, cols].bitcast(E5M2_X4),
+                        lhsT_scale=scales[:, c, cols],
+                        rhs=w_codes[:, w_cols].bitcast(E4M3_X4),
+                        rhs_scale=w_scales[:, w_cols],
+                        start=(e == 0),
+                        stop=(e == N_EMB - 1),
+                    )
+
         def empty_sums(sums):
             feature_rows = []
             for k in range(N_CHEB):
@@ -246,22 +265,17 @@ def tile_dygcn_pb_k_kernel(tc, x_g, emb, weights_pool, bias_pool, grad_out, out)
             b, s = divmod(half * HALF_TILES + i, 2)
             nc.sync.dma_start(out=out[b, :, s * P : (s + 1) * P, :].rearrange("k n f -> n k f"), in_=token_rows[:])
 
-        def store_last_half(sums):
-            first_copy = [nc.scalar.copy, nc.vector.tensor_copy, nc.scalar.copy]
-            second_copy = [nc.vector.tensor_copy, nc.scalar.copy, nc.vector.tensor_copy]
-            for k in range(N_CHEB):
-                rows = ring.tile([P, HALF], F32, name="feature_rows%d" % k, tag="feature_rows%d" % k, bufs=1)
-                first_copy[k](out=rows[:], in_=sums[k][:])
-                bank = turn_banks.tile([P, HALF_TILES, P], F32, tag="turn")
-                for i in range(HALF_TILES):
-                    nc.tensor.transpose(bank[:, i, :], rows[:, i * P : (i + 1) * P], identity[:])
-                token_rows = ring.tile([P, HALF_TILES, P], F32, tag="last_rows")
-                second_copy[k](out=token_rows[:], in_=bank[:])
-                for j in range(2):
-                    nc.sync.dma_start(
-                        out=out[2 + j, k, :, :].rearrange("(s n) f -> n s f", s=2),
-                        in_=token_rows[:, 2 * j : 2 * j + 2, :],
-                    )
+        def store_last_half(token_sums):
+            for i in range(HALF_TILES):
+                token_rows = ring.tile([P, N_CHEB, P], F32, tag="last_rows", bufs=4)
+                copy_out = nc.vector.tensor_copy if i % 2 == 0 else nc.scalar.copy
+                copy_out(
+                    out=token_rows[:].rearrange("p k f -> p (k f)"), in_=token_sums[i][:, : N_CHEB * P]
+                )
+                b, s = divmod(HALF_TILES + i, 2)
+                nc.sync.dma_start(
+                    out=out[b, :, s * P : (s + 1) * P, :].rearrange("k n f -> n k f"), in_=token_rows[:]
+                )
 
         loaded = {}
         for r in range(PE_SPREAD_ROUNDS, 1 + LOAD_AHEAD):
@@ -273,6 +287,9 @@ def tile_dygcn_pb_k_kernel(tc, x_g, emb, weights_pool, bias_pool, grad_out, out)
             half, pair = divmod(r, ROUNDS_PER_HALF)
             if pair == 0:
                 sums = [sum_banks.tile([P, HALF], F32, name="sum%d" % k, tag="sum%d" % k) for k in range(N_CHEB)]
+            if r == ROUNDS_PER_HALF:
+                fourth = turn_banks.tile([P, HALF], F32, tag="turn")
+                sums.append(fourth)
             gated, grouped_tiles, spread = prepared
             if r + 4 < ROUNDS_PER_HALF:
                 load_weights(r + 4)
@@ -287,7 +304,10 @@ def tile_dygcn_pb_k_kernel(tc, x_g, emb, weights_pool, bias_pool, grad_out, out)
             codes, scales = gate_and_quantise(half, gated, spread)
             if half == 0:
                 quantise_weights(pair, grouped_tiles)
-            multiply(pair, codes, scales, sums)
+            if half == 0:
+                multiply(pair, codes, scales, sums)
+            else:
+                multiply_by_tokens(pair, codes, scales, sums)
             if r == ROUNDS_PER_HALF - 1:
                 feature_rows = empty_sums(sums)
         store_last_half(sums)

@@ -98,8 +98,8 @@ def tile_dygcn_pb_k_kernel(tc, x_g, emb, weights_pool, bias_pool, grad_out, out)
             return [words[:, 0, :], words[:, 1, :]]
 
         g_cols = keep.tile([P, 2, VECTOR_TILES * P * PACK], BF16)
-        w_codes = keep.tile([P, (N_EMB * N_CHEB + 1) * P], U32, align_bytes=64)
-        w_scales = keep.tile([P, (N_EMB * N_CHEB + 1) * P], U8, align_bytes=64)
+        w_codes = keep.tile([P, (N_EMB * N_CHEB + 1) * P], U32, align_bytes=256)
+        w_scales = keep.tile([P, (N_EMB * N_CHEB + 1) * P], U8, align_bytes=256)
         nc.vector.memset(w_codes[:, N_EMB * N_CHEB * P :].bitcast(I32), 0)
         nc.vector.memset(w_scales[:, N_EMB * N_CHEB * P :].bitcast(I32), 0)
 
@@ -132,7 +132,7 @@ def tile_dygcn_pb_k_kernel(tc, x_g, emb, weights_pool, bias_pool, grad_out, out)
                     BF16,
                     tag="w_grouped",
                     bufs=2 * WEIGHT_BANKS_PER_ROUND,
-                    align_bytes=64,
+                    align_bytes=256,
                 )
                 nc.scalar.copy(
                     out=grouped[:].bitcast(F32).rearrange("p (c f u) -> p c f u", c=BLOCKS_PER_BANK, u=2),
@@ -189,7 +189,7 @@ def tile_dygcn_pb_k_kernel(tc, x_g, emb, weights_pool, bias_pool, grad_out, out)
 
         def prepare(r):
             half, pair = divmod(r, ROUNDS_PER_HALF)
-            gated = ring.tile([P, 2, HALF * PACK], BF16, tag="gated", align_bytes=64)
+            gated = ring.tile([P, 2, HALF * PACK], BF16, tag="gated", align_bytes=256)
             spread = spread_embedding(half, pair) if r < PE_SPREAD_ROUNDS else loaded[r]
             if pair == 0:
                 turn_gradient(half)
@@ -200,8 +200,8 @@ def tile_dygcn_pb_k_kernel(tc, x_g, emb, weights_pool, bias_pool, grad_out, out)
             return gated, grouped_tiles, spread
 
         def gate_and_quantise(half, gated, spread):
-            codes = ring.tile([P, 2, HALF], U32, tag="codes", align_bytes=64)
-            scales = ring.tile([P, 2, HALF], U8, tag="scales", align_bytes=64)
+            codes = ring.tile([P, 2, HALF], U32, tag="codes", align_bytes=256)
+            scales = ring.tile([P, 2, HALF], U8, tag="scales", align_bytes=256)
             for c in range(2):
                 nc.vector.tensor_tensor(
                     out=gated[:, c, : VECTOR_TILES * P * PACK].rearrange("p (t u i) -> p t u i", u=2, i=2),

from contextlib import ExitStack

import concourse.mybir as mybir
from concourse.masks import make_identity

BF16 = mybir.dt.bfloat16
F32 = mybir.dt.float32
U32 = mybir.dt.uint32
U8 = mybir.dt.uint8
I32 = mybir.dt.int32
E4M3_X4 = mybir.dt.float8_e4m3fn_x4
E5M2_X4 = mybir.dt.float8_e5m2_x4

P = 128
PACK = 4
N_EMB = 16
N_CHEB = 3
N_OUT = 512
N_TILES = 8
HALF_TILES = 4
HALF = HALF_TILES * P
VECTOR_TILES = 3
PE_SPREAD_ROUNDS = 5
LOAD_AHEAD = 3
ROUNDS_PER_HALF = N_EMB // 2
N_ROUNDS = 2 * ROUNDS_PER_HALF
BLOCKS_PER_BANK = 2
WEIGHT_BANKS_PER_ROUND = 3

FLOPS = 2 * 1024 * 384 * 8192
BYTES = 2 * (1024 * 16 + 16 * 3 * 128 * 512 + 1024 * 512) + 4 * 1024 * 384


def tile_dygcn_pb_k_kernel(tc, x_g, emb, weights_pool, bias_pool, grad_out, out):
    nc = tc.nc
    with ExitStack() as ctx:
        keep = ctx.enter_context(tc.tile_pool(name="keep", bufs=1))
        ring = ctx.enter_context(tc.tile_pool(name="ring", bufs=3))
        sum_banks = ctx.enter_context(tc.psum_pool(name="sum_banks", bufs=1))
        turn_banks = ctx.enter_context(tc.psum_pool(name="turn_banks", bufs=5))

        emb_rows = keep.tile([P, N_TILES * N_EMB], BF16)
        g_rows = keep.tile([P, N_TILES, N_OUT], BF16)
        w_rows = keep.tile([P, N_EMB * N_CHEB, N_OUT], BF16)
        g_view = grad_out.rearrange("b (s p) o -> p (b s) o", p=P)
        w_view = weights_pool.rearrange("e k f o -> f (e k) o")
        nc.sync.dma_start(
            out=emb_rows[:].rearrange("p (i e) -> p i e", e=N_EMB),
            in_=emb.rearrange("b (s p) e -> p (b s) e", p=P),
        )
        for i in range(HALF_TILES):
            nc.sync.dma_start(out=g_rows[:, i, :], in_=g_view[:, i, :])

        def load_weights(pair):
            blocks = slice(pair * 2 * N_CHEB, (pair + 1) * 2 * N_CHEB)
            nc.sync.dma_start(out=w_rows[:, blocks, :], in_=w_view[:, blocks, :])

        load_weights(0)

        identity = keep.tile([P, P], F32)
        make_identity(nc, identity[:])

        emb_pairs = keep.tile([P, N_TILES * N_EMB * 2], BF16)
        nc.vector.tensor_copy(
            out=emb_pairs[:].rearrange("p (c i) -> p c i", i=2),
            in_=emb_rows[:].unsqueeze(2).to_broadcast([P, N_TILES * N_EMB, 2]),
        )
        emb_words = emb_pairs[:].bitcast(F32)
        emb_scales = keep.tile([P, N_TILES * N_EMB], F32)
        nc.scalar.copy(out=emb_scales[:], in_=emb_rows[:])

        emb_pairs_by_e = keep.tile([P, N_EMB * N_TILES * 2], BF16)
        nc.vector.tensor_copy(
            out=emb_pairs_by_e[:].rearrange("p (e i w) -> p e i w", e=N_EMB, w=2),
            in_=emb_rows[:]
            .rearrange("p (i e) -> p e i", e=N_EMB)
            .unsqueeze(3)
            .to_broadcast([P, N_EMB, N_TILES, 2]),
        )
        emb_bank = turn_banks.tile([P, P], F32, tag="turn")
        nc.tensor.transpose(emb_bank[:], emb_pairs_by_e[:].bitcast(F32), identity[:])
        emb_cols = keep.tile([P, P], F32)
        nc.vector.tensor_copy(out=emb_cols[:], in_=emb_bank[:])
        parked = out[3, 2, P : 2 * P, :]
        nc.sync.dma_start(out=parked, in_=emb_cols[:])
        parked_by_e = parked.rearrange("(e i) t -> e i t", i=N_TILES)
        for pair in range(1, 4):
            load_weights(pair)

        def load_spread(r):
            half, pair = divmod(r, ROUNDS_PER_HALF)
            words = ring.tile([P, 2, VECTOR_TILES * P], F32, tag="spread_words", bufs=5)
            first = half * HALF_TILES
            nc.sync.dma_start(
                out=words[:].rearrange("p c (i t) -> p c i t", i=VECTOR_TILES),
                in_=parked_by_e[2 * pair : 2 * pair + 2, first : first + VECTOR_TILES, :].partition_broadcast(P),
            )
            return [words[:, 0, :], words[:, 1, :]]

        g_cols = keep.tile([P, 2, VECTOR_TILES * P * PACK], BF16)
        w_codes = keep.tile([P, (N_EMB * N_CHEB + 1) * P], U32, align_bytes=256)
        w_scales = keep.tile([P, (N_EMB * N_CHEB + 1) * P], U8, align_bytes=256)
        nc.vector.memset(w_codes[:, N_EMB * N_CHEB * P :].bitcast(I32), 0)
        nc.vector.memset(w_scales[:, N_EMB * N_CHEB * P :].bitcast(I32), 0)

        def turn_rows(bank, rows):
            words = rows.bitcast(F32)
            for u in range(2):
                nc.tensor.transpose(bank[:, u, :], words[:, u * P : (u + 1) * P], identity[:])

        def turn_gradient(half):
            for i in range(VECTOR_TILES):
                bank = turn_banks.tile([P, 2, P], F32, tag="turn")
                turn_rows(bank, g_rows[:, half * HALF_TILES + i, :])
                copy_out = nc.vector.tensor_copy if half == 0 else nc.scalar.copy
                copy_out(
                    out=g_cols[:, half, i * P * PACK : (i + 1) * P * PACK]
                    .bitcast(F32)
                    .rearrange("p (t u) -> p t u", u=2),
                    in_=bank[:].rearrange("p u t -> p t u"),
                )

        def turn_weights(pair):
            grouped_tiles = []
            for bank_index in range(WEIGHT_BANKS_PER_ROUND):
                bank = turn_banks.tile([P, BLOCKS_PER_BANK, 2, P], F32, tag="turn")
                for c in range(BLOCKS_PER_BANK):
                    block = (pair * WEIGHT_BANKS_PER_ROUND + bank_index) * BLOCKS_PER_BANK + c
                    turn_rows(bank[:, c], w_rows[:, block, :])
                grouped = ring.tile(
                    [P, BLOCKS_PER_BANK * P * PACK],
                    BF16,
                    tag="w_grouped",
                    bufs=2 * WEIGHT_BANKS_PER_ROUND,
                    align_bytes=256,
                )
                nc.scalar.copy(
                    out=grouped[:].bitcast(F32).rearrange("p (c f u) -> p c f u", c=BLOCKS_PER_BANK, u=2),
                    in_=bank[:].rearrange("p c u f -> p c f u"),
                )
                grouped_tiles.append(grouped)
            return grouped_tiles

        def quantise_weights(pair, grouped_tiles):
            for bank_index in range(WEIGHT_BANKS_PER_ROUND):
                first = (pair * WEIGHT_BANKS_PER_ROUND + bank_index) * BLOCKS_PER_BANK * P
                cols = slice(first, first + BLOCKS_PER_BANK * P)
                nc.vector.quantize_mx(
                    out=w_codes[:, cols].bitcast(E4M3_X4),
                    scales=w_scales[:, cols],
                    in_=grouped_tiles[bank_index][:],
                )

        def gate_on_scalar(half, pair, gated):
            for i in range(VECTOR_TILES, HALF_TILES):
                tile_index = half * HALF_TILES + i
                scaled = ring.tile([P, 2, N_OUT], BF16, tag="scaled")
                for c in range(2):
                    column = tile_index * N_EMB + 2 * pair + c
                    nc.scalar.activation(
                        out=scaled[:, c, :],
                        in_=g_rows[:, tile_index, :],
                        func=mybir.ActivationFunctionType.Copy,
                        scale=emb_scales[:, column : column + 1],
                    )
                bank = turn_banks.tile([P, 2, 2, P], F32, tag="turn")
                for c in range(2):
                    turn_rows(bank[:, c], scaled[:, c, :])
                nc.scalar.copy(
                    out=gated[:, :, i * P * PACK : (i + 1) * P * PACK]
                    .bitcast(F32)
                    .rearrange("p c (t u) -> p c t u", u=2),
                    in_=bank[:].rearrange("p c u t -> p c t u"),
                )

        def spread_embedding(half, pair):
            spread = []
            for c in range(2):
                bank = turn_banks.tile([P, VECTOR_TILES * P], F32, tag="turn")
                for i in range(VECTOR_TILES):
                    column = (half * HALF_TILES + i) * N_EMB + 2 * pair + c
                    nc.tensor.transpose(
                        bank[:, i * P : (i + 1) * P],
                        emb_words[:, column : column + 1].to_broadcast([P, P]),
                        identity[:],
                    )
                spread.append(bank[:])
            return spread

        def prepare(r):
            half, pair = divmod(r, ROUNDS_PER_HALF)
            gated = ring.tile([P, 2, HALF * PACK], BF16, tag="gated", align_bytes=256)
            spread = spread_embedding(half, pair) if r < PE_SPREAD_ROUNDS else loaded[r]
            if pair == 0:
                turn_gradient(half)
            gate_on_scalar(half, pair, gated)
            grouped_tiles = []
            if half == 0:
                grouped_tiles = turn_weights(pair)
            return gated, grouped_tiles, spread

        def gate_and_quantise(half, gated, spread):
            codes = ring.tile([P, 2, HALF], U32, tag="codes", align_bytes=256)
            scales = ring.tile([P, 2, HALF], U8, tag="scales", align_bytes=256)
            for c in range(2):
                nc.vector.tensor_tensor(
                    out=gated[:, c, : VECTOR_TILES * P * PACK].rearrange("p (t u i) -> p t u i", u=2, i=2),
                    in0=g_cols[:, half, :].rearrange("p (t u i) -> p t u i", u=2, i=2),
                    in1=spread[c]
                    .bitcast(BF16)
                    .rearrange("p (t i) -> p t i", i=2)
                    .unsqueeze(2)
                    .to_broadcast([P, VECTOR_TILES * P, 2, 2]),
                    op=mybir.AluOpType.mult,
                )
            for c in range(2):
                nc.vector.quantize_mx(out=codes[:, c, :].bitcast(E5M2_X4), scales=scales[:, c, :], in_=gated[:, c, :])
            return codes, scales

        def multiply(pair, codes, scales, sums):
            for c in range(2):
                e = 2 * pair + c
                for k in range(N_CHEB):
                    cols = slice((e * N_CHEB + k) * P, (e * N_CHEB + k + 1) * P)
                    nc.tensor.matmul_mx(
                        out=sums[k][:],
                        lhsT=w_codes[:, cols].bitcast(E4M3_X4),
                        lhsT_scale=w_scales[:, cols],
                        rhs=codes[:, c, :].bitcast(E5M2_X4),
                        rhs_scale=scales[:, c, :],
                        start=(e == 0),
                        stop=(e == N_EMB - 1),
                    )

        def multiply_by_tokens(pair, codes, scales, token_sums):
            for c in range(2):
                e = 2 * pair + c
                w_cols = slice(e * N_CHEB * P, (e * N_CHEB + PACK) * P)
                for i in range(HALF_TILES):
                    cols = slice(i * P, (i + 1) * P)
                    nc.tensor.matmul_mx(
                        out=token_sums[i][:],
                        lhsT=codes[:, c, cols].bitcast(E5M2_X4),
                        lhsT_scale=scales[:, c, cols],
                        rhs=w_codes[:, w_cols].bitcast(E4M3_X4),
                        rhs_scale=w_scales[:, w_cols],
                        start=(e == 0),
                        stop=(e == N_EMB - 1),
                    )

        def empty_sums(sums):
            feature_rows = []
            for k in range(N_CHEB):
                rows = ring.tile([P, HALF], F32, name="feature_rows%d" % k, tag="feature_rows%d" % k, bufs=1)
                nc.scalar.copy(out=rows[:], in_=sums[k][:])
                feature_rows.append(rows)
            return feature_rows

        def store_tile(half, i, feature_rows):
            bank = turn_banks.tile([P, N_CHEB, P], F32, tag="turn")
            for k in range(N_CHEB):
                nc.tensor.transpose(bank[:, k, :], feature_rows[k][:, i * P : (i + 1) * P], identity[:])
            token_rows = ring.tile([P, N_CHEB, P], F32, tag="token_rows")
            nc.scalar.copy(out=token_rows[:], in_=bank[:])
            b, s = divmod(half * HALF_TILES + i, 2)
            nc.sync.dma_start(out=out[b, :, s * P : (s + 1) * P, :].rearrange("k n f -> n k f"), in_=token_rows[:])

        def store_last_half(token_sums):
            for i in range(HALF_TILES):
                token_rows = ring.tile([P, N_CHEB, P], F32, tag="last_rows", bufs=4)
                copy_out = nc.vector.tensor_copy if i % 2 == 0 else nc.scalar.copy
                copy_out(
                    out=token_rows[:].rearrange("p k f -> p (k f)"), in_=token_sums[i][:, : N_CHEB * P]
                )
                b, s = divmod(HALF_TILES + i, 2)
                nc.sync.dma_start(
                    out=out[b, :, s * P : (s + 1) * P, :].rearrange("k n f -> n k f"), in_=token_rows[:]
                )

        loaded = {}
        for r in range(PE_SPREAD_ROUNDS, 1 + LOAD_AHEAD):
            loaded[r] = load_spread(r)
        prepared = prepare(0)
        sums = []
        feature_rows = []
        for r in range(N_ROUNDS):
            half, pair = divmod(r, ROUNDS_PER_HALF)
            if pair == 0:
                sums = [sum_banks.tile([P, HALF], F32, name="sum%d" % k, tag="sum%d" % k) for k in range(N_CHEB)]
            if r == ROUNDS_PER_HALF:
                fourth = turn_banks.tile([P, HALF], F32, tag="turn")
                sums.append(fourth)
            gated, grouped_tiles, spread = prepared
            if r + 4 < ROUNDS_PER_HALF:
                load_weights(r + 4)
            if r + 4 == ROUNDS_PER_HALF:
                nc.sync.dma_start(out=g_rows[:, HALF_TILES:, :], in_=g_view[:, HALF_TILES:, :])
            if PE_SPREAD_ROUNDS <= r + 1 + LOAD_AHEAD < N_ROUNDS:
                loaded[r + 1 + LOAD_AHEAD] = load_spread(r + 1 + LOAD_AHEAD)
            if r + 1 < N_ROUNDS:
                prepared = prepare(r + 1)
            if half == 1 and 1 <= pair <= HALF_TILES:
                store_tile(0, pair - 1, feature_rows)
            codes, scales = gate_and_quantise(half, gated, spread)
            if half == 0:
                quantise_weights(pair, grouped_tiles)
            if half == 0:
                multiply(pair, codes, scales, sums)
            else:
                multiply_by_tokens(pair, codes, scales, sums)
            if r == ROUNDS_PER_HALF - 1:
                feature_rows = empty_sums(sums)
        store_last_half(sums)
